import numpy as np
import ml_dtypes


def mxq(x, axis, fmt="e4m3"):
    dtype, down = {"e4m3": (ml_dtypes.float8_e4m3fn, 7), "e5m2": (ml_dtypes.float8_e5m2, 14)}[fmt]
    v = np.moveaxis(np.asarray(x, np.float32).astype(ml_dtypes.bfloat16).astype(np.float64), axis, -1)
    blocks = v.reshape(v.shape[:-1] + (-1, 32))
    amax = np.abs(blocks).max(-1, keepdims=True)
    byte = np.maximum(np.where(amax > 0, np.frexp(amax)[1] - 1 + 127, 0) - down, 1)
    scale = np.exp2(byte - 127.0)
    codes = (blocks / scale).astype(np.float32).astype(dtype).astype(np.float64)
    return np.moveaxis((codes * scale).reshape(v.shape), -1, axis)


WIDE = False


def mx_kscale(k):
    if not WIDE:
        return np.ones(k)
    levels = np.array([10, -10, 5, -5, 0])
    a = np.random.permutation(np.resize(levels, k // 512 * 4)).reshape(k // 512, 4)
    idx = np.arange(k)
    return np.exp2(a[idx // 512, idx % 128 // 32])


BF16 = ml_dtypes.bfloat16


def bf(x):
    return np.asarray(x, np.float32).astype(BF16)


def f64(x):
    return np.asarray(x).astype(np.float64)


B, N, D = 4, 256, 512
BN = B * N
DM = D + D


def sigmoid(v):
    return 1.0 / (1.0 + np.exp(-v))


def setup_inputs():
    s, t = mx_kscale(DM), mx_kscale(D)
    return {"node_state": bf(np.random.standard_normal((B, N, D)) * t),
            "message": bf(np.random.standard_normal((B, N, DM)) * s),
            "w_r": bf(np.random.standard_normal((DM, D)) / np.sqrt(DM) / s[:, None]),
            "u_r": bf(np.random.standard_normal((D, D)) / np.sqrt(D) / t[:, None]),
            "w": bf(np.random.standard_normal((DM, D)) / np.sqrt(DM) / s[:, None]),
            "u": bf(np.random.standard_normal((D, D)) / np.sqrt(D) / t[:, None])}


def reference(node_state, message, w_r, u_r, w, u):
    h = f64(node_state).reshape(BN, D)
    m = f64(message).reshape(BN, DM)
    mq = mxq(m, 1, "e4m3")
    r_t = sigmoid((mq @ mxq(f64(w_r), 0, "e4m3")) + (mxq(h, 1, "e4m3") @ mxq(f64(u_r), 0, "e4m3")))
    return np.tanh((mq @ mxq(f64(w), 0, "e4m3")) + (mxq(r_t * h, 1, "e4m3") @ mxq(f64(u), 0, "e4m3")))

@@ -1,0 +1,237 @@
+from contextlib import ExitStack
+
+import concourse.masks as masks
+import concourse.mybir as mybir
+
+F32 = mybir.dt.float32
+BF16 = mybir.dt.bfloat16
+U32 = mybir.dt.uint32
+U8 = mybir.dt.uint8
+FP8X4 = mybir.dt.float8_e4m3fn_x4
+SIGMOID = mybir.ActivationFunctionType.Sigmoid
+TANH = mybir.ActivationFunctionType.Tanh
+MULT = mybir.AluOpType.mult
+
+P = 128
+PACK = 4
+K_PASS = P * PACK
+ROWS = 1024
+D = 512
+DM = 1024
+M_PASSES = DM // K_PASS
+ROW_TILES = ROWS // P
+GROUP_TILES = 2
+GROUPS = ROW_TILES // GROUP_TILES
+GROUP_ROWS = GROUP_TILES * P
+HALF = K_PASS // 2
+
+FLOPS = 2 * ROWS * D * (DM + D + DM + D)
+
+
+def tile_updatefunction_pa_kernel(tc, node_state, message, w_r, u_r, w, u, out):
+    nc = tc.nc
+    with ExitStack() as ctx:
+        keep = ctx.enter_context(tc.tile_pool(name="keep", bufs=1))
+        banks = ctx.enter_context(tc.psum_pool(name="banks", bufs=8))
+
+        m_rows = message.flatten_outer_dims().rearrange("(p i) k -> p i k", i=ROW_TILES)
+        h_rows = node_state.flatten_outer_dims().rearrange("(p i) k -> p i k", i=ROW_TILES)
+        out_rows = out.rearrange("(p i) d -> p i d", i=ROW_TILES)
+
+        warm = keep.tile([P, 1], F32, name="warm")
+        nc.vector.memset(warm[:], 0.0)
+        warm_out = keep.tile([P, 1], F32, name="warm_out")
+        nc.scalar.activation(out=warm_out[:], in_=warm[:], func=SIGMOID)
+
+        ident = keep.tile([P, P], F32, name="ident")
+        masks.make_identity(nc, ident[:])
+
+        def load_weight(name, rows):
+            raw = keep.tile([P, PACK, D], BF16, name="raw_" + name)
+            nc.sync.dma_start(
+                out=raw[:].rearrange("p (u e) c -> p u e c", u=2),
+                in_=rows.rearrange("(u p e) c -> p u e c", u=2, e=2),
+            )
+            return raw
+
+        def load_group(name, rows, g, width):
+            raw = keep.tile([P, GROUP_TILES, width], BF16, name="%s_raw%d" % (name, g))
+            nc.sync.dma_start(out=raw[:], in_=rows[:, g * GROUP_TILES : (g + 1) * GROUP_TILES, :])
+            return raw
+
+        raw_w = {}
+        m_raw = {}
+        h_raw = {}
+        raw_w["w_r0"] = load_weight("w_r0", w_r[0:K_PASS, :])
+        m_raw[0] = load_group("m", m_rows, 0, DM)
+        raw_w["w_r1"] = load_weight("w_r1", w_r[K_PASS : 2 * K_PASS, :])
+        h_raw[0] = load_group("h", h_rows, 0, D)
+        raw_w["u_r"] = load_weight("u_r", u_r)
+        m_raw[1] = load_group("m", m_rows, 1, DM)
+        raw_w["w0"] = load_weight("w0", w[0:K_PASS, :])
+        h_raw[1] = load_group("h", h_rows, 1, D)
+        raw_w["w1"] = load_weight("w1", w[K_PASS : 2 * K_PASS, :])
+        m_raw[2] = load_group("m", m_rows, 2, DM)
+        raw_w["u"] = load_weight("u", u)
+        h_raw[2] = load_group("h", h_rows, 2, D)
+        m_raw[3] = load_group("m", m_rows, 3, DM)
+        h_raw[3] = load_group("h", h_rows, 3, D)
+
+        w_codes = {}
+        w_scales = {}
+
+        def quantise_weight(name, copy, gate_order):
+            raw = raw_w[name]
+            grouped = keep.tile([P, D, PACK], BF16, name="grouped_" + name, align_bytes=64)
+            if gate_order:
+                for half in range(2):
+                    cols = slice(half * HALF, (half + 1) * HALF)
+                    copy(
+                        out=grouped[:, cols, :].rearrange("p (e q) t -> p q e t", e=2),
+                        in_=raw[:, :, cols].rearrange("p t (q e) -> p q e t", e=2),
+                    )
+            else:
+                copy(
+                    out=grouped[:].rearrange("p (c i) t -> p c t i", i=4),
+                    in_=raw[:].rearrange("p t (c i) -> p c t i", i=4),
+                )
+            codes = keep.tile([P, D], U32, name="codes_" + name, align_bytes=64)
+            scales = keep.tile([P, D], U8, name="scales_" + name, align_bytes=64)
+            nc.vector.quantize_mx(
+                out=codes[:].bitcast(FP8X4),
+                scales=scales[:],
+                in_=grouped[:].rearrange("p c t -> p (c t)"),
+            )
+            w_codes[name] = codes
+            w_scales[name] = scales
+
+        m_codes = {}
+        m_scales = {}
+        h_codes = {}
+        h_scales = {}
+        h_grouped = {}
+
+        def transpose_pass(raw_words, first_word, grouped_words):
+            flipped = banks.tile([P, 2, GROUP_ROWS], F32, name="flipped", tag="bank")
+            for j in range(GROUP_TILES):
+                for half in range(2):
+                    start = first_word + half * P
+                    nc.tensor.transpose(
+                        flipped[:, half, j * P : (j + 1) * P],
+                        raw_words[:, j, start : start + P],
+                        ident[:],
+                    )
+            nc.scalar.copy(out=grouped_words, in_=flipped[:].rearrange("p u r -> p r u"))
+
+        def prepare_inputs(g):
+            mg = keep.tile([P, M_PASSES * GROUP_ROWS * PACK], BF16, name="m_grouped%d" % g, align_bytes=64)
+            mg_words = mg[:].bitcast(F32).rearrange("p (c r u) -> p c r u", c=M_PASSES, u=2)
+            for c in range(M_PASSES):
+                transpose_pass(m_raw[g][:].bitcast(F32), c * 2 * P, mg_words[:, c, :, :])
+            hg = keep.tile([P, GROUP_ROWS * PACK], BF16, name="h_grouped%d" % g, align_bytes=64)
+            hg_words = hg[:].bitcast(F32).rearrange("p (r u) -> p r u", u=2)
+            transpose_pass(h_raw[g][:].bitcast(F32), 0, hg_words)
+
+            mc = keep.tile([P, M_PASSES, GROUP_ROWS], U32, name="m_codes%d" % g, align_bytes=64)
+            ms = keep.tile([P, M_PASSES, GROUP_ROWS], U8, name="m_scales%d" % g, align_bytes=64)
+            nc.vector.quantize_mx(
+                out=mc[:].rearrange("p c r -> p (c r)").bitcast(FP8X4),
+                scales=ms[:].rearrange("p c r -> p (c r)"),
+                in_=mg[:],
+            )
+            hc = keep.tile([P, GROUP_ROWS], U32, name="h_codes%d" % g, align_bytes=64)
+            hs = keep.tile([P, GROUP_ROWS], U8, name="h_scales%d" % g, align_bytes=64)
+            nc.vector.quantize_mx(out=hc[:].bitcast(FP8X4), scales=hs[:], in_=hg[:])
+            m_codes[g], m_scales[g], h_codes[g], h_scales[g], h_grouped[g] = mc, ms, hc, hs, hg
+
+        rh_codes = {}
+        rh_scales = {}
+
+        def gate(g):
+            r = keep.tile([P, PACK, GROUP_ROWS], F32, name="r%d" % g)
+            for half in range(2):
+                acc = banks.tile([P, 2, GROUP_ROWS], F32, name="gate_acc", tag="bank")
+                for e in range(2):
+                    t = 2 * half + e
+                    feats = slice(t * P, (t + 1) * P)
+                    for c in range(M_PASSES):
+                        name = "w_r%d" % c
+                        nc.tensor.matmul_mx(
+                            out=acc[:, e, :],
+                            lhsT=w_codes[name][:, feats].bitcast(FP8X4),
+                            lhsT_scale=w_scales[name][:, feats],
+                            rhs=m_codes[g][:, c, :].bitcast(FP8X4),
+                            rhs_scale=m_scales[g][:, c, :],
+                            start=(c == 0),
+                            stop=False,
+                        )
+                    nc.tensor.matmul_mx(
+                        out=acc[:, e, :],
+                        lhsT=w_codes["u_r"][:, feats].bitcast(FP8X4),
+                        lhsT_scale=w_scales["u_r"][:, feats],
+                        rhs=h_codes[g][:].bitcast(FP8X4),
+                        rhs_scale=h_scales[g][:],
+                        start=False,
+                        stop=True,
+                    )
+                nc.scalar.activation(out=r[:, 2 * half : 2 * half + 2, :], in_=acc[:], func=SIGMOID)
+            rh = keep.tile([P, GROUP_ROWS, PACK], BF16, name="rh%d" % g, align_bytes=64)
+            nc.vector.tensor_tensor(
+                out=rh[:],
+                in0=r[:].rearrange("p t r -> p r t"),
+                in1=h_grouped[g][:].rearrange("p (r t) -> p r t", t=PACK),
+                op=MULT,
+            )
+            rc = keep.tile([P, GROUP_ROWS], U32, name="rh_codes%d" % g, align_bytes=64)
+            rs = keep.tile([P, GROUP_ROWS], U8, name="rh_scales%d" % g, align_bytes=64)
+            nc.vector.quantize_mx(
+                out=rc[:].bitcast(FP8X4), scales=rs[:], in_=rh[:].rearrange("p r t -> p (r t)")
+            )
+            rh_codes[g], rh_scales[g] = rc, rs
+
+        def candidate(g):
+            for j in range(GROUP_TILES):
+                rows = slice(j * P, (j + 1) * P)
+                acc = banks.tile([P, D], F32, name="cand_acc", tag="bank")
+                for c in range(M_PASSES):
+                    name = "w%d" % c
+                    nc.tensor.matmul_mx(
+                        out=acc[:],
+                        lhsT=m_codes[g][:, c, rows].bitcast(FP8X4),
+                        lhsT_scale=m_scales[g][:, c, rows],
+                        rhs=w_codes[name][:].bitcast(FP8X4),
+                        rhs_scale=w_scales[name][:],
+                        start=(c == 0),
+                        stop=False,
+                    )
+                nc.tensor.matmul_mx(
+                    out=acc[:],
+                    lhsT=rh_codes[g][:, rows].bitcast(FP8X4),
+                    lhsT_scale=rh_scales[g][:, rows],
+                    rhs=w_codes["u"][:].bitcast(FP8X4),
+                    rhs_scale=w_scales["u"][:],
+                    start=False,
+                    stop=True,
+                )
+                result = keep.tile([P, D], F32, name="result%d_%d" % (g, j))
+                nc.scalar.activation(out=result[:], in_=acc[:], func=TANH)
+                nc.sync.dma_start(out=out_rows[:, g * GROUP_TILES + j, :], in_=result[:])
+
+        quantise_weight("w_r0", nc.vector.tensor_copy, True)
+        prepare_inputs(0)
+        quantise_weight("w_r1", nc.vector.tensor_copy, True)
+        quantise_weight("u_r", nc.vector.tensor_copy, True)
+        prepare_inputs(1)
+        gate(0)
+        quantise_weight("w0", nc.vector.tensor_copy, False)
+        prepare_inputs(2)
+        gate(1)
+        quantise_weight("w1", nc.vector.tensor_copy, False)
+        quantise_weight("u", nc.scalar.copy, False)
+        prepare_inputs(3)
+        candidate(0)
+        gate(2)
+        candidate(1)
+        gate(3)
+        candidate(2)
+        candidate(3)

@@ -15,6 +15,7 @@ MULT = mybir.AluOpType.mult
 P = 128
 PACK = 4
 K_PASS = P * PACK
+HALF = K_PASS // 2
 ROWS = 1024
 D = 512
 DM = 1024
@@ -23,7 +24,7 @@ ROW_TILES = ROWS // P
 GROUP_TILES = 2
 GROUPS = ROW_TILES // GROUP_TILES
 GROUP_ROWS = GROUP_TILES * P
-HALF = K_PASS // 2
+PSUM_BANKS = 8
 
 FLOPS = 2 * ROWS * D * (DM + D + DM + D)
 
@@ -32,206 +33,196 @@ def tile_updatefunction_pa_kernel(tc, node_state, message, w_r, u_r, w, u, out):
     nc = tc.nc
     with ExitStack() as ctx:
         keep = ctx.enter_context(tc.tile_pool(name="keep", bufs=1))
-        banks = ctx.enter_context(tc.psum_pool(name="banks", bufs=8))
+        banks = ctx.enter_context(tc.psum_pool(name="banks", bufs=PSUM_BANKS))
+        ctx.enter_context(tc.manual_schedule())
 
         m_rows = message.flatten_outer_dims().rearrange("(p i) k -> p i k", i=ROW_TILES)
         h_rows = node_state.flatten_outer_dims().rearrange("(p i) k -> p i k", i=ROW_TILES)
         out_rows = out.rearrange("(p i) d -> p i d", i=ROW_TILES)
 
+        zero = keep.tile([P, 1], F32, name="zero")
+        nc.vector.memset(zero[:], 0.0)
         warm = keep.tile([P, 1], F32, name="warm")
-        nc.vector.memset(warm[:], 0.0)
-        warm_out = keep.tile([P, 1], F32, name="warm_out")
-        nc.scalar.activation(out=warm_out[:], in_=warm[:], func=SIGMOID)
+        nc.scalar.activation(out=warm[:], in_=zero[:], func=SIGMOID)
 
         ident = keep.tile([P, P], F32, name="ident")
         masks.make_identity(nc, ident[:])
 
+        raw = {}
+
         def load_weight(name, rows):
-            raw = keep.tile([P, PACK, D], BF16, name="raw_" + name)
+            raw[name] = keep.tile([P, PACK, D], BF16, name="raw_" + name)
             nc.sync.dma_start(
-                out=raw[:].rearrange("p (u e) c -> p u e c", u=2),
+                out=raw[name][:].rearrange("p (u e) c -> p u e c", u=2),
                 in_=rows.rearrange("(u p e) c -> p u e c", u=2, e=2),
             )
-            return raw
 
-        def load_group(name, rows, g, width):
-            raw = keep.tile([P, GROUP_TILES, width], BF16, name="%s_raw%d" % (name, g))
-            nc.sync.dma_start(out=raw[:], in_=rows[:, g * GROUP_TILES : (g + 1) * GROUP_TILES, :])
-            return raw
-
-        raw_w = {}
-        m_raw = {}
-        h_raw = {}
-        raw_w["w_r0"] = load_weight("w_r0", w_r[0:K_PASS, :])
-        m_raw[0] = load_group("m", m_rows, 0, DM)
-        raw_w["w_r1"] = load_weight("w_r1", w_r[K_PASS : 2 * K_PASS, :])
-        h_raw[0] = load_group("h", h_rows, 0, D)
-        raw_w["u_r"] = load_weight("u_r", u_r)
-        m_raw[1] = load_group("m", m_rows, 1, DM)
-        raw_w["w0"] = load_weight("w0", w[0:K_PASS, :])
-        h_raw[1] = load_group("h", h_rows, 1, D)
-        raw_w["w1"] = load_weight("w1", w[K_PASS : 2 * K_PASS, :])
-        m_raw[2] = load_group("m", m_rows, 2, DM)
-        raw_w["u"] = load_weight("u", u)
-        h_raw[2] = load_group("h", h_rows, 2, D)
-        m_raw[3] = load_group("m", m_rows, 3, DM)
-        h_raw[3] = load_group("h", h_rows, 3, D)
-
-        w_codes = {}
-        w_scales = {}
-
-        def quantise_weight(name, copy, gate_order):
-            raw = raw_w[name]
-            grouped = keep.tile([P, D, PACK], BF16, name="grouped_" + name, align_bytes=64)
-            if gate_order:
-                for half in range(2):
-                    cols = slice(half * HALF, (half + 1) * HALF)
-                    copy(
-                        out=grouped[:, cols, :].rearrange("p (e q) t -> p q e t", e=2),
-                        in_=raw[:, :, cols].rearrange("p t (q e) -> p q e t", e=2),
-                    )
-            else:
-                copy(
-                    out=grouped[:].rearrange("p (c i) t -> p c t i", i=4),
-                    in_=raw[:].rearrange("p t (c i) -> p c t i", i=4),
-                )
-            codes = keep.tile([P, D], U32, name="codes_" + name, align_bytes=64)
-            scales = keep.tile([P, D], U8, name="scales_" + name, align_bytes=64)
-            nc.vector.quantize_mx(
-                out=codes[:].bitcast(FP8X4),
-                scales=scales[:],
-                in_=grouped[:].rearrange("p c t -> p (c t)"),
+        def load_rows(name, rows, g, width):
+            raw[name, g] = keep.tile([P, GROUP_TILES, width], BF16, name="raw_%s%d" % (name, g))
+            nc.sync.dma_start(
+                out=raw[name, g][:], in_=rows[:, g * GROUP_TILES : (g + 1) * GROUP_TILES, :]
             )
-            w_codes[name] = codes
-            w_scales[name] = scales
 
-        m_codes = {}
-        m_scales = {}
-        h_codes = {}
-        h_scales = {}
-        h_grouped = {}
+        load_weight("w_r0", w_r[0:K_PASS, :])
+        load_rows("m", m_rows, 0, DM)
+        load_weight("w_r1", w_r[K_PASS : 2 * K_PASS, :])
+        load_rows("h", h_rows, 0, D)
+        load_weight("u_r", u_r)
+        load_rows("m", m_rows, 1, DM)
+        load_rows("h", h_rows, 1, D)
+        load_weight("w0", w[0:K_PASS, :])
+        load_rows("m", m_rows, 2, DM)
+        load_rows("h", h_rows, 2, D)
+        load_weight("w1", w[K_PASS : 2 * K_PASS, :])
+        load_rows("m", m_rows, 3, DM)
+        load_rows("h", h_rows, 3, D)
+        load_weight("u", u)
 
-        def transpose_pass(raw_words, first_word, grouped_words):
+        grouped = {}
+        codes = {}
+        scales = {}
+
+        def operand_tiles(key, name, words):
+            grouped[key] = keep.tile([P, words * PACK], BF16, name="grouped_" + name, align_bytes=64)
+            codes[key] = keep.tile([P, words], U32, name="codes_" + name, align_bytes=64)
+            scales[key] = keep.tile([P, words], U8, name="scales_" + name, align_bytes=64)
+
+        def quantise(key, first_word, words):
+            cols = slice(first_word, first_word + words)
+            nc.vector.quantize_mx(
+                out=codes[key][:, cols].bitcast(FP8X4),
+                scales=scales[key][:, cols],
+                in_=grouped[key][:, first_word * PACK : (first_word + words) * PACK],
+            )
+
+        for name in ("w_r0", "w_r1", "u_r", "w0", "w1", "u"):
+            operand_tiles(name, name, D)
+        for g in range(GROUPS):
+            operand_tiles(("m", g), "m%d" % g, M_PASSES * GROUP_ROWS)
+            operand_tiles(("h", g), "h%d" % g, GROUP_ROWS)
+            operand_tiles(("rh", g), "rh%d" % g, GROUP_ROWS)
+
+        def regroup_gate_weight(name):
+            for half, copy in ((0, nc.vector.tensor_copy), (1, nc.scalar.copy)):
+                cols = slice(half * HALF, (half + 1) * HALF)
+                copy(
+                    out=grouped[name][:, half * HALF * PACK : (half + 1) * HALF * PACK].rearrange(
+                        "p (e q t) -> p q e t", e=2, t=PACK
+                    ),
+                    in_=raw[name][:, :, cols].rearrange("p t (q e) -> p q e t", e=2),
+                )
+
+        def quantise_gate_weight(name):
+            for half in range(2):
+                quantise(name, half * HALF, HALF)
+
+        def regroup_candidate_weight(name):
+            nc.vector.tensor_copy(
+                out=grouped[name][:].rearrange("p (c i t) -> p c t i", i=4, t=PACK),
+                in_=raw[name][:].rearrange("p t (c i) -> p c t i", i=4),
+            )
+
+        def flip(source, first_word, target_words):
             flipped = banks.tile([P, 2, GROUP_ROWS], F32, name="flipped", tag="bank")
+            words = source[:].bitcast(F32)
             for j in range(GROUP_TILES):
                 for half in range(2):
                     start = first_word + half * P
                     nc.tensor.transpose(
-                        flipped[:, half, j * P : (j + 1) * P],
-                        raw_words[:, j, start : start + P],
-                        ident[:],
+                        flipped[:, half, j * P : (j + 1) * P], words[:, j, start : start + P], ident[:]
                     )
-            nc.scalar.copy(out=grouped_words, in_=flipped[:].rearrange("p u r -> p r u"))
-
-        def prepare_inputs(g):
-            mg = keep.tile([P, M_PASSES * GROUP_ROWS * PACK], BF16, name="m_grouped%d" % g, align_bytes=64)
-            mg_words = mg[:].bitcast(F32).rearrange("p (c r u) -> p c r u", c=M_PASSES, u=2)
-            for c in range(M_PASSES):
-                transpose_pass(m_raw[g][:].bitcast(F32), c * 2 * P, mg_words[:, c, :, :])
-            hg = keep.tile([P, GROUP_ROWS * PACK], BF16, name="h_grouped%d" % g, align_bytes=64)
-            hg_words = hg[:].bitcast(F32).rearrange("p (r u) -> p r u", u=2)
-            transpose_pass(h_raw[g][:].bitcast(F32), 0, hg_words)
-
-            mc = keep.tile([P, M_PASSES, GROUP_ROWS], U32, name="m_codes%d" % g, align_bytes=64)
-            ms = keep.tile([P, M_PASSES, GROUP_ROWS], U8, name="m_scales%d" % g, align_bytes=64)
-            nc.vector.quantize_mx(
-                out=mc[:].rearrange("p c r -> p (c r)").bitcast(FP8X4),
-                scales=ms[:].rearrange("p c r -> p (c r)"),
-                in_=mg[:],
+            nc.scalar.copy(
+                out=target_words.rearrange("p (r u) -> p r u", u=2),
+                in_=flipped[:].rearrange("p u r -> p r u"),
             )
-            hc = keep.tile([P, GROUP_ROWS], U32, name="h_codes%d" % g, align_bytes=64)
-            hs = keep.tile([P, GROUP_ROWS], U8, name="h_scales%d" % g, align_bytes=64)
-            nc.vector.quantize_mx(out=hc[:].bitcast(FP8X4), scales=hs[:], in_=hg[:])
-            m_codes[g], m_scales[g], h_codes[g], h_scales[g], h_grouped[g] = mc, ms, hc, hs, hg
 
-        rh_codes = {}
-        rh_scales = {}
+        def flip_message(g):
+            words = grouped["m", g][:].bitcast(F32)
+            for c in range(M_PASSES):
+                flip(raw["m", g], c * HALF, words[:, c * 2 * GROUP_ROWS : (c + 1) * 2 * GROUP_ROWS])
 
-        def gate(g):
-            r = keep.tile([P, PACK, GROUP_ROWS], F32, name="r%d" % g)
+        def flip_state(g):
+            flip(raw["h", g], 0, grouped["h", g][:].bitcast(F32))
+
+        def quantise_inputs(g):
+            quantise(("m", g), 0, M_PASSES * GROUP_ROWS)
+            quantise(("h", g), 0, GROUP_ROWS)
+
+        gate = {}
+
+        def mx_pass(acc, stationary, s_cols, moving, m_cols, start, stop):
+            nc.tensor.matmul_mx(
+                out=acc,
+                lhsT=codes[stationary][:, s_cols].bitcast(FP8X4),
+                lhsT_scale=scales[stationary][:, s_cols],
+                rhs=codes[moving][:, m_cols].bitcast(FP8X4),
+                rhs_scale=scales[moving][:, m_cols],
+                start=start,
+                stop=stop,
+            )
+
+        def gate_of(g):
+            gate[g] = keep.tile([P, 2, GROUP_ROWS, 2], F32, name="gate%d" % g)
             for half in range(2):
                 acc = banks.tile([P, 2, GROUP_ROWS], F32, name="gate_acc", tag="bank")
                 for e in range(2):
-                    t = 2 * half + e
-                    feats = slice(t * P, (t + 1) * P)
+                    feats = slice((2 * half + e) * P, (2 * half + e + 1) * P)
                     for c in range(M_PASSES):
-                        name = "w_r%d" % c
-                        nc.tensor.matmul_mx(
-                            out=acc[:, e, :],
-                            lhsT=w_codes[name][:, feats].bitcast(FP8X4),
-                            lhsT_scale=w_scales[name][:, feats],
-                            rhs=m_codes[g][:, c, :].bitcast(FP8X4),
-                            rhs_scale=m_scales[g][:, c, :],
-                            start=(c == 0),
-                            stop=False,
-                        )
-                    nc.tensor.matmul_mx(
-                        out=acc[:, e, :],
-                        lhsT=w_codes["u_r"][:, feats].bitcast(FP8X4),
-                        lhsT_scale=w_scales["u_r"][:, feats],
-                        rhs=h_codes[g][:].bitcast(FP8X4),
-                        rhs_scale=h_scales[g][:],
-                        start=False,
-                        stop=True,
-                    )
-                nc.scalar.activation(out=r[:, 2 * half : 2 * half + 2, :], in_=acc[:], func=SIGMOID)
-            rh = keep.tile([P, GROUP_ROWS, PACK], BF16, name="rh%d" % g, align_bytes=64)
+                        rows = slice(c * GROUP_ROWS, (c + 1) * GROUP_ROWS)
+                        mx_pass(acc[:, e, :], "w_r%d" % c, feats, ("m", g), rows, c == 0, False)
+                    mx_pass(acc[:, e, :], "u_r", feats, ("h", g), slice(0, GROUP_ROWS), False, True)
+                nc.scalar.activation(
+                    out=gate[g][:, half, :, :], in_=acc[:].rearrange("p e r -> p r e"), func=SIGMOID
+                )
+
+        def multiply(g):
             nc.vector.tensor_tensor(
-                out=rh[:],
-                in0=r[:].rearrange("p t r -> p r t"),
-                in1=h_grouped[g][:].rearrange("p (r t) -> p r t", t=PACK),
+                out=grouped["rh", g][:].rearrange("p (r u e) -> p r u e", u=2, e=2),
+                in0=gate[g][:].rearrange("p u r e -> p r u e"),
+                in1=grouped["h", g][:].rearrange("p (r u e) -> p r u e", u=2, e=2),
                 op=MULT,
             )
-            rc = keep.tile([P, GROUP_ROWS], U32, name="rh_codes%d" % g, align_bytes=64)
-            rs = keep.tile([P, GROUP_ROWS], U8, name="rh_scales%d" % g, align_bytes=64)
-            nc.vector.quantize_mx(
-                out=rc[:].bitcast(FP8X4), scales=rs[:], in_=rh[:].rearrange("p r t -> p (r t)")
-            )
-            rh_codes[g], rh_scales[g] = rc, rs
 
-        def candidate(g):
+        def candidate_of(g):
             for j in range(GROUP_TILES):
-                rows = slice(j * P, (j + 1) * P)
                 acc = banks.tile([P, D], F32, name="cand_acc", tag="bank")
                 for c in range(M_PASSES):
-                    name = "w%d" % c
-                    nc.tensor.matmul_mx(
-                        out=acc[:],
-                        lhsT=m_codes[g][:, c, rows].bitcast(FP8X4),
-                        lhsT_scale=m_scales[g][:, c, rows],
-                        rhs=w_codes[name][:].bitcast(FP8X4),
-                        rhs_scale=w_scales[name][:],
-                        start=(c == 0),
-                        stop=False,
-                    )
-                nc.tensor.matmul_mx(
-                    out=acc[:],
-                    lhsT=rh_codes[g][:, rows].bitcast(FP8X4),
-                    lhsT_scale=rh_scales[g][:, rows],
-                    rhs=w_codes["u"][:].bitcast(FP8X4),
-                    rhs_scale=w_scales["u"][:],
-                    start=False,
-                    stop=True,
-                )
+                    rows = slice(c * GROUP_ROWS + j * P, c * GROUP_ROWS + (j + 1) * P)
+                    mx_pass(acc[:], ("m", g), rows, "w%d" % c, slice(0, D), c == 0, False)
+                mx_pass(acc[:], ("rh", g), slice(j * P, (j + 1) * P), "u", slice(0, D), False, True)
                 result = keep.tile([P, D], F32, name="result%d_%d" % (g, j))
                 nc.scalar.activation(out=result[:], in_=acc[:], func=TANH)
                 nc.sync.dma_start(out=out_rows[:, g * GROUP_TILES + j, :], in_=result[:])
 
-        quantise_weight("w_r0", nc.vector.tensor_copy, True)
-        prepare_inputs(0)
-        quantise_weight("w_r1", nc.vector.tensor_copy, True)
-        quantise_weight("u_r", nc.vector.tensor_copy, True)
-        prepare_inputs(1)
-        gate(0)
-        quantise_weight("w0", nc.vector.tensor_copy, False)
-        prepare_inputs(2)
-        gate(1)
-        quantise_weight("w1", nc.vector.tensor_copy, False)
-        quantise_weight("u", nc.scalar.copy, False)
-        prepare_inputs(3)
-        candidate(0)
-        gate(2)
-        candidate(1)
-        gate(3)
-        candidate(2)
-        candidate(3)
+        regroup_gate_weight("w_r0")
+        flip_message(0)
+        regroup_gate_weight("w_r1")
+        quantise_gate_weight("w_r0")
+        flip_state(0)
+        quantise(("m", 0), 0, M_PASSES * GROUP_ROWS)
+        regroup_gate_weight("u_r")
+        quantise_gate_weight("w_r1")
+        quantise(("h", 0), 0, GROUP_ROWS)
+        quantise_gate_weight("u_r")
+        flip_message(1)
+        flip_state(1)
+
+        candidate_weights = ("w0", "w1", "u")
+        for i in range(GROUPS + 3):
+            if i + 1 < GROUPS:
+                quantise_inputs(i + 1)
+            if i < GROUPS:
+                gate_of(i)
+            if i + 2 < GROUPS:
+                flip_message(i + 2)
+                flip_state(i + 2)
+            if i < len(candidate_weights):
+                regroup_candidate_weight(candidate_weights[i])
+            if 0 <= i - 2 < GROUPS:
+                quantise(("rh", i - 2), 0, GROUP_ROWS)
+            if i < len(candidate_weights):
+                quantise(candidate_weights[i], 0, D)
+            if 0 <= i - 1 < GROUPS:
+                multiply(i - 1)
+            if 0 <= i - 3 < GROUPS:
+                candidate_of(i - 3)

@@ -183,15 +183,21 @@ def tile_updatefunction_pa_kernel(tc, node_state, message, w_r, u_r, w, u, out):
                 op=MULT,
             )
 
-        def candidate_of(g):
+        cand_acc = {}
+
+        def open_candidate(g):
             for j in range(GROUP_TILES):
-                acc = banks.tile([P, D], F32, name="cand_acc", tag="bank")
+                cand_acc[g, j] = banks.tile([P, D], F32, name="cand_acc", tag="bank")
                 for c in range(M_PASSES):
                     rows = slice(c * GROUP_ROWS + j * P, c * GROUP_ROWS + (j + 1) * P)
-                    mx_pass(acc[:], ("m", g), rows, "w%d" % c, slice(0, D), c == 0, False)
-                mx_pass(acc[:], ("rh", g), slice(j * P, (j + 1) * P), "u", slice(0, D), False, True)
+                    mx_pass(cand_acc[g, j][:], ("m", g), rows, "w%d" % c, slice(0, D), c == 0, False)
+
+        def close_candidate(g):
+            for j in range(GROUP_TILES):
+                rows = slice(j * P, (j + 1) * P)
+                mx_pass(cand_acc[g, j][:], ("rh", g), rows, "u", slice(0, D), False, True)
                 result = keep.tile([P, D], F32, name="result%d_%d" % (g, j))
-                nc.scalar.activation(out=result[:], in_=acc[:], func=TANH)
+                nc.scalar.activation(out=result[:], in_=cand_acc[g, j][:], func=TANH)
                 nc.sync.dma_start(out=out_rows[:, g * GROUP_TILES + j, :], in_=result[:])
 
         regroup_gate_weight("w_r0")
@@ -224,5 +230,7 @@ def tile_updatefunction_pa_kernel(tc, node_state, message, w_r, u_r, w, u, out):
                 quantise(candidate_weights[i], 0, D)
             if 0 <= i - 1 < GROUPS:
                 multiply(i - 1)
+            if 0 <= i - 2 < GROUPS:
+                open_candidate(i - 2)
             if 0 <= i - 3 < GROUPS:
-                candidate_of(i - 3)
+                close_candidate(i - 3)

@@ -25,6 +25,7 @@ GROUP_TILES = 2
 GROUPS = ROW_TILES // GROUP_TILES
 GROUP_ROWS = GROUP_TILES * P
 PSUM_BANKS = 8
+WARM_UP_MATMULS = 4
 
 FLOPS = 2 * ROWS * D * (DM + D + DM + D)
 
@@ -47,6 +48,14 @@ def tile_updatefunction_pa_kernel(tc, node_state, message, w_r, u_r, w, u, out):
 
         ident = keep.tile([P, P], F32, name="ident")
         masks.make_identity(nc, ident[:])
+
+        zeros = keep.tile([P, D], BF16, name="zeros")
+        nc.vector.memset(zeros[:], 0.0)
+
+        def warm_up_tensor_engine():
+            for n in range(WARM_UP_MATMULS):
+                unread = banks.tile([P, D], F32, name="unread", tag="bank")
+                nc.tensor.matmul(unread[:], lhsT=zeros[:, 0:P], rhs=zeros[:], start=True, stop=True)
 
         raw = {}
 
@@ -185,26 +194,25 @@ def tile_updatefunction_pa_kernel(tc, node_state, message, w_r, u_r, w, u, out):
 
         cand_acc = {}
 
-        def open_candidate(g):
-            for j in range(GROUP_TILES):
-                cand_acc[g, j] = banks.tile([P, D], F32, name="cand_acc", tag="bank")
-                for c in range(M_PASSES):
-                    rows = slice(c * GROUP_ROWS + j * P, c * GROUP_ROWS + (j + 1) * P)
-                    mx_pass(cand_acc[g, j][:], ("m", g), rows, "w%d" % c, slice(0, D), c == 0, False)
+        def open_candidate(g, j):
+            cand_acc[g, j] = banks.tile([P, D], F32, name="cand_acc", tag="bank")
+            for c in range(M_PASSES):
+                rows = slice(c * GROUP_ROWS + j * P, c * GROUP_ROWS + (j + 1) * P)
+                mx_pass(cand_acc[g, j][:], ("m", g), rows, "w%d" % c, slice(0, D), c == 0, False)
 
-        def close_candidate(g):
-            for j in range(GROUP_TILES):
-                rows = slice(j * P, (j + 1) * P)
-                mx_pass(cand_acc[g, j][:], ("rh", g), rows, "u", slice(0, D), False, True)
-                result = keep.tile([P, D], F32, name="result%d_%d" % (g, j))
-                nc.scalar.activation(out=result[:], in_=cand_acc[g, j][:], func=TANH)
-                nc.sync.dma_start(out=out_rows[:, g * GROUP_TILES + j, :], in_=result[:])
+        def close_candidate(g, j):
+            rows = slice(j * P, (j + 1) * P)
+            mx_pass(cand_acc[g, j][:], ("rh", g), rows, "u", slice(0, D), False, True)
+            result = keep.tile([P, D], F32, name="result%d_%d" % (g, j))
+            nc.scalar.activation(out=result[:], in_=cand_acc[g, j][:], func=TANH)
+            nc.sync.dma_start(out=out_rows[:, g * GROUP_TILES + j, :], in_=result[:])
 
         regroup_gate_weight("w_r0")
         flip_message(0)
-        regroup_gate_weight("w_r1")
         quantise_gate_weight("w_r0")
+        regroup_gate_weight("w_r1")
         flip_state(0)
+        warm_up_tensor_engine()
         quantise(("m", 0), 0, M_PASSES * GROUP_ROWS)
         regroup_gate_weight("u_r")
         quantise_gate_weight("w_r1")
@@ -230,7 +238,8 @@ def tile_updatefunction_pa_kernel(tc, node_state, message, w_r, u_r, w, u, out):
                 quantise(candidate_weights[i], 0, D)
             if 0 <= i - 1 < GROUPS:
                 multiply(i - 1)
-            if 0 <= i - 2 < GROUPS:
-                open_candidate(i - 2)
-            if 0 <= i - 3 < GROUPS:
-                close_candidate(i - 3)
+            for j in range(GROUP_TILES):
+                if 0 <= i - 2 < GROUPS:
+                    open_candidate(i - 2, j)
+                if 0 <= i - 3 < GROUPS:
+                    close_candidate(i - 3, j)

@@ -25,7 +25,7 @@ GROUP_TILES = 2
 GROUPS = ROW_TILES // GROUP_TILES
 GROUP_ROWS = GROUP_TILES * P
 PSUM_BANKS = 8
-WARM_UP_MATMULS = 4
+WARM_UP_MATMULS = 2
 
 FLOPS = 2 * ROWS * D * (DM + D + DM + D)
 
@@ -121,14 +121,12 @@ def tile_updatefunction_pa_kernel(tc, node_state, message, w_r, u_r, w, u, out):
                     in_=raw[name][:, :, cols].rearrange("p t (q e) -> p q e t", e=2),
                 )
 
-        def quantise_gate_weight(name):
-            for half in range(2):
-                quantise(name, half * HALF, HALF)
-
-        def regroup_candidate_weight(name):
-            nc.vector.tensor_copy(
-                out=grouped[name][:].rearrange("p (c i t) -> p c t i", i=4, t=PACK),
-                in_=raw[name][:].rearrange("p t (c i) -> p c t i", i=4),
+        def regroup_candidate_weight(name, copy, first_col, cols):
+            copy(
+                out=grouped[name][:, first_col * PACK : (first_col + cols) * PACK].rearrange(
+                    "p (c i t) -> p c t i", i=4, t=PACK
+                ),
+                in_=raw[name][:, :, first_col : first_col + cols].rearrange("p t (c i) -> p c t i", i=4),
             )
 
         def flip(source, first_word, target_words):
@@ -158,6 +156,8 @@ def tile_updatefunction_pa_kernel(tc, node_state, message, w_r, u_r, w, u, out):
             quantise(("h", g), 0, GROUP_ROWS)
 
         gate = {}
+        gate_acc = {}
+        issued = set()
 
         def mx_pass(acc, stationary, s_cols, moving, m_cols, start, stop):
             nc.tensor.matmul_mx(
@@ -170,76 +170,110 @@ def tile_updatefunction_pa_kernel(tc, node_state, message, w_r, u_r, w, u, out):
                 stop=stop,
             )
 
-        def gate_of(g):
-            gate[g] = keep.tile([P, 2, GROUP_ROWS, 2], F32, name="gate%d" % g)
-            for half in range(2):
-                acc = banks.tile([P, 2, GROUP_ROWS], F32, name="gate_acc", tag="bank")
-                for e in range(2):
-                    feats = slice((2 * half + e) * P, (2 * half + e + 1) * P)
-                    for c in range(M_PASSES):
-                        rows = slice(c * GROUP_ROWS, (c + 1) * GROUP_ROWS)
-                        mx_pass(acc[:, e, :], "w_r%d" % c, feats, ("m", g), rows, c == 0, False)
-                    mx_pass(acc[:, e, :], "u_r", feats, ("h", g), slice(0, GROUP_ROWS), False, True)
-                nc.scalar.activation(
-                    out=gate[g][:, half, :, :], in_=acc[:].rearrange("p e r -> p r e"), func=SIGMOID
-                )
+        def gate_pass(g, half, e, c):
+            if (g, half) not in gate_acc:
+                gate_acc[g, half] = banks.tile([P, 2, GROUP_ROWS], F32, name="gate_acc", tag="bank")
+            feats = slice((2 * half + e) * P, (2 * half + e + 1) * P)
+            acc = gate_acc[g, half][:, e, :]
+            if c < M_PASSES:
+                rows = slice(c * GROUP_ROWS, (c + 1) * GROUP_ROWS)
+                mx_pass(acc, "w_r%d" % c, feats, ("m", g), rows, c == 0, False)
+            else:
+                mx_pass(acc, "u_r", feats, ("h", g), slice(0, GROUP_ROWS), False, True)
+            issued.add((g, half, e, c))
 
-        def multiply(g):
+        def finish_gate(g, half):
+            if g not in gate:
+                gate[g] = keep.tile([P, 2, GROUP_ROWS, 2], F32, name="gate%d" % g)
+            for e in range(2):
+                for c in range(M_PASSES + 1):
+                    if (g, half, e, c) not in issued:
+                        gate_pass(g, half, e, c)
+            nc.scalar.activation(
+                out=gate[g][:, half, :, :],
+                in_=gate_acc[g, half][:].rearrange("p e r -> p r e"),
+                func=SIGMOID,
+            )
+
+        def multiply(g, first_row, rows):
+            cols = slice(first_row * PACK, (first_row + rows) * PACK)
             nc.vector.tensor_tensor(
-                out=grouped["rh", g][:].rearrange("p (r u e) -> p r u e", u=2, e=2),
-                in0=gate[g][:].rearrange("p u r e -> p r u e"),
-                in1=grouped["h", g][:].rearrange("p (r u e) -> p r u e", u=2, e=2),
+                out=grouped["rh", g][:, cols].rearrange("p (r u e) -> p r u e", u=2, e=2),
+                in0=gate[g][:, :, first_row : first_row + rows, :].rearrange("p u r e -> p r u e"),
+                in1=grouped["h", g][:, cols].rearrange("p (r u e) -> p r u e", u=2, e=2),
                 op=MULT,
             )
 
+        def gated_state(g):
+            for j in range(GROUP_TILES):
+                multiply(g, j * P, P)
+            for j in range(GROUP_TILES):
+                quantise(("rh", g), j * P, P)
+
         cand_acc = {}
 
-        def open_candidate(g, j):
-            cand_acc[g, j] = banks.tile([P, D], F32, name="cand_acc", tag="bank")
+        def open_candidate(n):
+            g, j = divmod(n, GROUP_TILES)
+            cand_acc[n] = banks.tile([P, D], F32, name="cand_acc", tag="bank")
             for c in range(M_PASSES):
                 rows = slice(c * GROUP_ROWS + j * P, c * GROUP_ROWS + (j + 1) * P)
-                mx_pass(cand_acc[g, j][:], ("m", g), rows, "w%d" % c, slice(0, D), c == 0, False)
+                mx_pass(cand_acc[n][:], ("m", g), rows, "w%d" % c, slice(0, D), c == 0, False)
 
-        def close_candidate(g, j):
+        def close_candidate(n):
+            g, j = divmod(n, GROUP_TILES)
             rows = slice(j * P, (j + 1) * P)
-            mx_pass(cand_acc[g, j][:], ("rh", g), rows, "u", slice(0, D), False, True)
-            result = keep.tile([P, D], F32, name="result%d_%d" % (g, j))
-            nc.scalar.activation(out=result[:], in_=cand_acc[g, j][:], func=TANH)
-            nc.sync.dma_start(out=out_rows[:, g * GROUP_TILES + j, :], in_=result[:])
+            mx_pass(cand_acc[n][:], ("rh", g), rows, "u", slice(0, D), False, True)
+            result = keep.tile([P, D], F32, name="result%d" % n)
+            nc.scalar.activation(out=result[:], in_=cand_acc[n][:], func=TANH)
+            nc.sync.dma_start(out=out_rows[:, n, :], in_=result[:])
 
         regroup_gate_weight("w_r0")
         flip_message(0)
-        quantise_gate_weight("w_r0")
+        quantise("w_r0", 0, HALF)
+        quantise("w_r0", HALF, HALF)
         regroup_gate_weight("w_r1")
         flip_state(0)
         warm_up_tensor_engine()
         quantise(("m", 0), 0, M_PASSES * GROUP_ROWS)
+        gate_pass(0, 0, 0, 0)
+        gate_pass(0, 1, 0, 0)
+        quantise("w_r1", 0, HALF)
+        gate_pass(0, 0, 0, 1)
         regroup_gate_weight("u_r")
-        quantise_gate_weight("w_r1")
+        quantise("w_r1", HALF, HALF)
         quantise(("h", 0), 0, GROUP_ROWS)
-        quantise_gate_weight("u_r")
+        quantise("u_r", 0, HALF)
         flip_message(1)
         flip_state(1)
+        quantise("u_r", HALF, HALF)
 
-        candidate_weights = ("w0", "w1", "u")
-        for i in range(GROUPS + 3):
-            if i + 1 < GROUPS:
-                quantise_inputs(i + 1)
-            if i < GROUPS:
-                gate_of(i)
+        for i in range(GROUPS - 1):
+            finish_gate(i, 0)
+            finish_gate(i, 1)
             if i + 2 < GROUPS:
                 flip_message(i + 2)
                 flip_state(i + 2)
-            if i < len(candidate_weights):
-                regroup_candidate_weight(candidate_weights[i])
-            if 0 <= i - 2 < GROUPS:
-                quantise(("rh", i - 2), 0, GROUP_ROWS)
-            if i < len(candidate_weights):
-                quantise(candidate_weights[i], 0, D)
-            if 0 <= i - 1 < GROUPS:
-                multiply(i - 1)
-            for j in range(GROUP_TILES):
-                if 0 <= i - 2 < GROUPS:
-                    open_candidate(i - 2, j)
-                if 0 <= i - 3 < GROUPS:
-                    close_candidate(i - 3, j)
+                regroup_candidate_weight("w%d" % i, nc.vector.tensor_copy, 0, D)
+                quantise_inputs(i + 1)
+                quantise("w%d" % i, 0, D)
+            if i == 1:
+                multiply(0, 0, GROUP_ROWS)
+                regroup_candidate_weight("u", nc.scalar.copy, HALF, HALF)
+        quantise_inputs(GROUPS - 1)
+        open_candidate(0)
+        open_candidate(1)
+        regroup_candidate_weight("u", nc.vector.tensor_copy, 0, HALF)
+        quantise(("rh", 0), 0, GROUP_ROWS)
+        quantise("u", 0, D)
+        finish_gate(GROUPS - 1, 0)
+        finish_gate(GROUPS - 1, 1)
+        for g in range(1, GROUPS):
+            gated_state(g)
+
+        last = ROW_TILES - 1
+        for n in range(ROW_TILES):
+            if n == last:
+                open_candidate(last)
+            close_candidate(n)
+            if n + 2 < last:
+                open_candidate(n + 2)

@@ -129,6 +129,14 @@ def tile_updatefunction_pa_kernel(tc, node_state, message, w_r, u_r, w, u, out):
                 in_=raw[name][:, :, first_col : first_col + cols].rearrange("p t (c i) -> p c t i", i=4),
             )
 
+        def regroup_plainly(name, copy, first_col, cols):
+            copy(
+                out=grouped[name][:, first_col * PACK : (first_col + cols) * PACK].rearrange(
+                    "p (c t) -> p c t", t=PACK
+                ),
+                in_=raw[name][:, :, first_col : first_col + cols].rearrange("p t c -> p c t"),
+            )
+
         def flip(source, first_word, target_words):
             flipped = banks.tile([P, 2, GROUP_ROWS], F32, name="flipped", tag="bank")
             words = source[:].bitcast(F32)
@@ -258,7 +266,7 @@ def tile_updatefunction_pa_kernel(tc, node_state, message, w_r, u_r, w, u, out):
                 quantise("w%d" % i, 0, D)
             if i == 1:
                 multiply(0, 0, GROUP_ROWS)
-                regroup_candidate_weight("u", nc.scalar.copy, HALF, HALF)
+                regroup_plainly("u", nc.scalar.copy, HALF, HALF)
         quantise_inputs(GROUPS - 1)
         open_candidate(0)
         open_candidate(1)

@@ -235,6 +235,19 @@ def tile_updatefunction_pa_kernel(tc, node_state, message, w_r, u_r, w, u, out):
             nc.scalar.activation(out=result[:], in_=cand_acc[n][:], func=TANH)
             nc.sync.dma_start(out=out_rows[:, n, :], in_=result[:])
 
+        def last_candidate(n):
+            g, j = divmod(n, GROUP_TILES)
+            for half in range(2):
+                cols = slice(half * HALF, (half + 1) * HALF)
+                acc = banks.tile([P, HALF], F32, name="half_acc", tag="bank")
+                for c in range(M_PASSES):
+                    rows = slice(c * GROUP_ROWS + j * P, c * GROUP_ROWS + (j + 1) * P)
+                    mx_pass(acc[:], ("m", g), rows, "w%d" % c, cols, c == 0, False)
+                mx_pass(acc[:], ("rh", g), slice(j * P, (j + 1) * P), "u", cols, False, True)
+                result = keep.tile([P, HALF], F32, name="result%d_%d" % (n, half))
+                nc.scalar.activation(out=result[:], in_=acc[:], func=TANH)
+                nc.sync.dma_start(out=out_rows[:, n, cols], in_=result[:])
+
         regroup_gate_weight("w_r0")
         flip_message(0)
         quantise("w_r0", 0, HALF)
@@ -279,9 +292,8 @@ def tile_updatefunction_pa_kernel(tc, node_state, message, w_r, u_r, w, u, out):
             gated_state(g)
 
         last = ROW_TILES - 1
-        for n in range(ROW_TILES):
-            if n == last:
-                open_candidate(last)
+        for n in range(last):
             close_candidate(n)
             if n + 2 < last:
                 open_candidate(n + 2)
+        last_candidate(last)

@@ -92,9 +92,9 @@ def tile_updatefunction_pa_kernel(tc, node_state, message, w_r, u_r, w, u, out):
         scales = {}
 
         def operand_tiles(key, name, words):
-            grouped[key] = keep.tile([P, words * PACK], BF16, name="grouped_" + name, align_bytes=64)
-            codes[key] = keep.tile([P, words], U32, name="codes_" + name, align_bytes=64)
-            scales[key] = keep.tile([P, words], U8, name="scales_" + name, align_bytes=64)
+            grouped[key] = keep.tile([P, words * PACK], BF16, name="grouped_" + name, align_bytes=256)
+            codes[key] = keep.tile([P, words], U32, name="codes_" + name, align_bytes=256)
+            scales[key] = keep.tile([P, words], U8, name="scales_" + name, align_bytes=256)
 
         def quantise(key, first_word, words):
             cols = slice(first_word, first_word + words)

@@ -46,7 +46,7 @@ def tile_updatefunction_pa_kernel(tc, node_state, message, w_r, u_r, w, u, out):
         warm = keep.tile([P, 1], F32, name="warm")
         nc.scalar.activation(out=warm[:], in_=zero[:], func=SIGMOID)
 
-        ident = keep.tile([P, P], F32, name="ident")
+        ident = keep.tile([P, P], F32, name="ident", align_bytes=256)
         masks.make_identity(nc, ident[:])
 
         zeros = keep.tile([P, D], BF16, name="zeros")
@@ -60,14 +60,16 @@ def tile_updatefunction_pa_kernel(tc, node_state, message, w_r, u_r, w, u, out):
         raw = {}
 
         def load_weight(name, rows):
-            raw[name] = keep.tile([P, PACK, D], BF16, name="raw_" + name)
+            raw[name] = keep.tile([P, PACK, D], BF16, name="raw_" + name, align_bytes=256)
             nc.sync.dma_start(
                 out=raw[name][:].rearrange("p (u e) c -> p u e c", u=2),
                 in_=rows.rearrange("(u p e) c -> p u e c", u=2, e=2),
             )
 
         def load_rows(name, rows, g, width):
-            raw[name, g] = keep.tile([P, GROUP_TILES, width], BF16, name="raw_%s%d" % (name, g))
+            raw[name, g] = keep.tile(
+                [P, GROUP_TILES, width], BF16, name="raw_%s%d" % (name, g), align_bytes=256
+            )
             nc.sync.dma_start(
                 out=raw[name, g][:], in_=rows[:, g * GROUP_TILES : (g + 1) * GROUP_TILES, :]
             )
@@ -192,7 +194,7 @@ def tile_updatefunction_pa_kernel(tc, node_state, message, w_r, u_r, w, u, out):
 
         def finish_gate(g, half):
             if g not in gate:
-                gate[g] = keep.tile([P, 2, GROUP_ROWS, 2], F32, name="gate%d" % g)
+                gate[g] = keep.tile([P, 2, GROUP_ROWS, 2], F32, name="gate%d" % g, align_bytes=256)
             for e in range(2):
                 for c in range(M_PASSES + 1):
                     if (g, half, e, c) not in issued:

@@ -46,7 +46,7 @@ def tile_updatefunction_pa_kernel(tc, node_state, message, w_r, u_r, w, u, out):
         warm = keep.tile([P, 1], F32, name="warm")
         nc.scalar.activation(out=warm[:], in_=zero[:], func=SIGMOID)
 
-        ident = keep.tile([P, P], F32, name="ident", align_bytes=256)
+        ident = keep.tile([P, P], F32, name="ident", align_bytes=512)
         masks.make_identity(nc, ident[:])
 
         zeros = keep.tile([P, D], BF16, name="zeros")
@@ -60,7 +60,7 @@ def tile_updatefunction_pa_kernel(tc, node_state, message, w_r, u_r, w, u, out):
         raw = {}
 
         def load_weight(name, rows):
-            raw[name] = keep.tile([P, PACK, D], BF16, name="raw_" + name, align_bytes=256)
+            raw[name] = keep.tile([P, PACK, D], BF16, name="raw_" + name, align_bytes=512)
             nc.sync.dma_start(
                 out=raw[name][:].rearrange("p (u e) c -> p u e c", u=2),
                 in_=rows.rearrange("(u p e) c -> p u e c", u=2, e=2),
@@ -68,7 +68,7 @@ def tile_updatefunction_pa_kernel(tc, node_state, message, w_r, u_r, w, u, out):
 
         def load_rows(name, rows, g, width):
             raw[name, g] = keep.tile(
-                [P, GROUP_TILES, width], BF16, name="raw_%s%d" % (name, g), align_bytes=256
+                [P, GROUP_TILES, width], BF16, name="raw_%s%d" % (name, g), align_bytes=512
             )
             nc.sync.dma_start(
                 out=raw[name, g][:], in_=rows[:, g * GROUP_TILES : (g + 1) * GROUP_TILES, :]
@@ -94,9 +94,9 @@ def tile_updatefunction_pa_kernel(tc, node_state, message, w_r, u_r, w, u, out):
         scales = {}
 
         def operand_tiles(key, name, words):
-            grouped[key] = keep.tile([P, words * PACK], BF16, name="grouped_" + name, align_bytes=256)
-            codes[key] = keep.tile([P, words], U32, name="codes_" + name, align_bytes=256)
-            scales[key] = keep.tile([P, words], U8, name="scales_" + name, align_bytes=256)
+            grouped[key] = keep.tile([P, words * PACK], BF16, name="grouped_" + name, align_bytes=512)
+            codes[key] = keep.tile([P, words], U32, name="codes_" + name, align_bytes=512)
+            scales[key] = keep.tile([P, words], U8, name="scales_" + name, align_bytes=512)
 
         def quantise(key, first_word, words):
             cols = slice(first_word, first_word + words)
@@ -194,7 +194,7 @@ def tile_updatefunction_pa_kernel(tc, node_state, message, w_r, u_r, w, u, out):
 
         def finish_gate(g, half):
             if g not in gate:
-                gate[g] = keep.tile([P, 2, GROUP_ROWS, 2], F32, name="gate%d" % g, align_bytes=256)
+                gate[g] = keep.tile([P, 2, GROUP_ROWS, 2], F32, name="gate%d" % g, align_bytes=512)
             for e in range(2):
                 for c in range(M_PASSES + 1):
                     if (g, half, e, c) not in issued:

@@ -37,9 +37,9 @@ def tile_updatefunction_pa_kernel(tc, node_state, message, w_r, u_r, w, u, out):
         banks = ctx.enter_context(tc.psum_pool(name="banks", bufs=PSUM_BANKS))
         ctx.enter_context(tc.manual_schedule())
 
-        m_rows = message.flatten_outer_dims().rearrange("(p i) k -> p i k", i=ROW_TILES)
-        h_rows = node_state.flatten_outer_dims().rearrange("(p i) k -> p i k", i=ROW_TILES)
-        out_rows = out.rearrange("(p i) d -> p i d", i=ROW_TILES)
+        m_rows = message.flatten_outer_dims().rearrange("(g p j) k -> p g j k", g=GROUPS, j=GROUP_TILES)
+        h_rows = node_state.flatten_outer_dims().rearrange("(g p j) k -> p g j k", g=GROUPS, j=GROUP_TILES)
+        out_rows = out.rearrange("(g p j) d -> p g j d", g=GROUPS, j=GROUP_TILES)
 
         zero = keep.tile([P, 1], F32, name="zero")
         nc.vector.memset(zero[:], 0.0)
@@ -71,7 +71,7 @@ def tile_updatefunction_pa_kernel(tc, node_state, message, w_r, u_r, w, u, out):
                 [P, GROUP_TILES, width], BF16, name="raw_%s%d" % (name, g), align_bytes=512
             )
             nc.sync.dma_start(
-                out=raw[name, g][:], in_=rows[:, g * GROUP_TILES : (g + 1) * GROUP_TILES, :]
+                out=raw[name, g][:], in_=rows[:, g, :, :]
             )
 
         load_weight("w_r0", w_r[0:K_PASS, :])
@@ -235,7 +235,7 @@ def tile_updatefunction_pa_kernel(tc, node_state, message, w_r, u_r, w, u, out):
             mx_pass(cand_acc[n][:], ("rh", g), rows, "u", slice(0, D), False, True)
             result = keep.tile([P, D], F32, name="result%d" % n)
             nc.scalar.activation(out=result[:], in_=cand_acc[n][:], func=TANH)
-            nc.sync.dma_start(out=out_rows[:, n, :], in_=result[:])
+            nc.sync.dma_start(out=out_rows[:, g, j, :], in_=result[:])
 
         def last_candidate(n):
             g, j = divmod(n, GROUP_TILES)
@@ -248,7 +248,7 @@ def tile_updatefunction_pa_kernel(tc, node_state, message, w_r, u_r, w, u, out):
                 mx_pass(acc[:], ("rh", g), slice(j * P, (j + 1) * P), "u", cols, False, True)
                 result = keep.tile([P, HALF], F32, name="result%d_%d" % (n, half))
                 nc.scalar.activation(out=result[:], in_=acc[:], func=TANH)
-                nc.sync.dma_start(out=out_rows[:, n, cols], in_=result[:])
+                nc.sync.dma_start(out=out_rows[:, g, j, cols], in_=result[:])
 
         regroup_gate_weight("w_r0")
         flip_message(0)

@@ -26,6 +26,7 @@ GROUPS = ROW_TILES // GROUP_TILES
 GROUP_ROWS = GROUP_TILES * P
 PSUM_BANKS = 8
 WARM_UP_MATMULS = 2
+EARLY_WARM_UP_MATMULS = 6
 
 FLOPS = 2 * ROWS * D * (DM + D + DM + D)
 
@@ -52,8 +53,8 @@ def tile_updatefunction_pa_kernel(tc, node_state, message, w_r, u_r, w, u, out):
         zeros = keep.tile([P, D], BF16, name="zeros")
         nc.vector.memset(zeros[:], 0.0)
 
-        def warm_up_tensor_engine():
-            for n in range(WARM_UP_MATMULS):
+        def warm_up_tensor_engine(matmuls):
+            for n in range(matmuls):
                 unread = banks.tile([P, D], F32, name="unread", tag="bank")
                 nc.tensor.matmul(unread[:], lhsT=zeros[:, 0:P], rhs=zeros[:], start=True, stop=True)
 
@@ -250,13 +251,14 @@ def tile_updatefunction_pa_kernel(tc, node_state, message, w_r, u_r, w, u, out):
                 nc.scalar.activation(out=result[:], in_=acc[:], func=TANH)
                 nc.sync.dma_start(out=out_rows[:, g, j, cols], in_=result[:])
 
+        warm_up_tensor_engine(EARLY_WARM_UP_MATMULS)
         regroup_gate_weight("w_r0")
         flip_message(0)
         quantise("w_r0", 0, HALF)
         quantise("w_r0", HALF, HALF)
         regroup_gate_weight("w_r1")
         flip_state(0)
-        warm_up_tensor_engine()
+        warm_up_tensor_engine(WARM_UP_MATMULS)
         quantise(("m", 0), 0, M_PASSES * GROUP_ROWS)
         gate_pass(0, 0, 0, 0)
         gate_pass(0, 1, 0, 0)

@@ -257,6 +257,7 @@ def tile_updatefunction_pa_kernel(tc, node_state, message, w_r, u_r, w, u, out):
         quantise("w_r0", 0, HALF)
         quantise("w_r0", HALF, HALF)
         regroup_gate_weight("w_r1")
+        warm_up_tensor_engine(WARM_UP_MATMULS)
         flip_state(0)
         warm_up_tensor_engine(WARM_UP_MATMULS)
         quantise(("m", 0), 0, M_PASSES * GROUP_ROWS)
@@ -268,6 +269,7 @@ def tile_updatefunction_pa_kernel(tc, node_state, message, w_r, u_r, w, u, out):
         quantise("w_r1", HALF, HALF)
         quantise(("h", 0), 0, GROUP_ROWS)
         quantise("u_r", 0, HALF)
+        warm_up_tensor_engine(WARM_UP_MATMULS + 1)
         flip_message(1)
         flip_state(1)
         quantise("u_r", HALF, HALF)

from contextlib import ExitStack

import concourse.masks as masks
import concourse.mybir as mybir

F32 = mybir.dt.float32
BF16 = mybir.dt.bfloat16
U32 = mybir.dt.uint32
U8 = mybir.dt.uint8
FP8X4 = mybir.dt.float8_e4m3fn_x4
SIGMOID = mybir.ActivationFunctionType.Sigmoid
TANH = mybir.ActivationFunctionType.Tanh
MULT = mybir.AluOpType.mult

P = 128
PACK = 4
K_PASS = P * PACK
HALF = K_PASS // 2
ROWS = 1024
D = 512
DM = 1024
M_PASSES = DM // K_PASS
ROW_TILES = ROWS // P
GROUP_TILES = 2
GROUPS = ROW_TILES // GROUP_TILES
GROUP_ROWS = GROUP_TILES * P
PSUM_BANKS = 8
WARM_UP_MATMULS = 2
EARLY_WARM_UP_MATMULS = 6

FLOPS = 2 * ROWS * D * (DM + D + DM + D)


def tile_updatefunction_pa_kernel(tc, node_state, message, w_r, u_r, w, u, out):
    nc = tc.nc
    with ExitStack() as ctx:
        keep = ctx.enter_context(tc.tile_pool(name="keep", bufs=1))
        banks = ctx.enter_context(tc.psum_pool(name="banks", bufs=PSUM_BANKS))
        ctx.enter_context(tc.manual_schedule())

        m_rows = message.flatten_outer_dims().rearrange("(g p j) k -> p g j k", g=GROUPS, j=GROUP_TILES)
        h_rows = node_state.flatten_outer_dims().rearrange("(g p j) k -> p g j k", g=GROUPS, j=GROUP_TILES)
        out_rows = out.rearrange("(g p j) d -> p g j d", g=GROUPS, j=GROUP_TILES)

        zero = keep.tile([P, 1], F32, name="zero")
        nc.vector.memset(zero[:], 0.0)
        warm = keep.tile([P, 1], F32, name="warm")
        nc.scalar.activation(out=warm[:], in_=zero[:], func=SIGMOID)

        ident = keep.tile([P, P], F32, name="ident", align_bytes=512)
        masks.make_identity(nc, ident[:])

        zeros = keep.tile([P, D], BF16, name="zeros")
        nc.vector.memset(zeros[:], 0.0)

        def warm_up_tensor_engine(matmuls):
            for n in range(matmuls):
                unread = banks.tile([P, D], F32, name="unread", tag="bank")
                nc.tensor.matmul(unread[:], lhsT=zeros[:, 0:P], rhs=zeros[:], start=True, stop=True)

        raw = {}

        def load_weight(name, rows):
            raw[name] = keep.tile([P, PACK, D], BF16, name="raw_" + name, align_bytes=512)
            nc.sync.dma_start(
                out=raw[name][:].rearrange("p (u e) c -> p u e c", u=2),
                in_=rows.rearrange("(u p e) c -> p u e c", u=2, e=2),
            )

        def load_rows(name, rows, g, width):
            raw[name, g] = keep.tile(
                [P, GROUP_TILES, width], BF16, name="raw_%s%d" % (name, g), align_bytes=512
            )
            nc.sync.dma_start(
                out=raw[name, g][:], in_=rows[:, g, :, :]
            )

        load_weight("w_r0", w_r[0:K_PASS, :])
        load_rows("m", m_rows, 0, DM)
        load_weight("w_r1", w_r[K_PASS : 2 * K_PASS, :])
        load_rows("h", h_rows, 0, D)
        load_weight("u_r", u_r)
        load_rows("m", m_rows, 1, DM)
        load_rows("h", h_rows, 1, D)
        load_weight("w0", w[0:K_PASS, :])
        load_rows("m", m_rows, 2, DM)
        load_rows("h", h_rows, 2, D)
        load_weight("w1", w[K_PASS : 2 * K_PASS, :])
        load_rows("m", m_rows, 3, DM)
        load_rows("h", h_rows, 3, D)
        load_weight("u", u)

        grouped = {}
        codes = {}
        scales = {}

        def operand_tiles(key, name, words):
            grouped[key] = keep.tile([P, words * PACK], BF16, name="grouped_" + name, align_bytes=512)
            codes[key] = keep.tile([P, words], U32, name="codes_" + name, align_bytes=512)
            scales[key] = keep.tile([P, words], U8, name="scales_" + name, align_bytes=512)

        def quantise(key, first_word, words):
            cols = slice(first_word, first_word + words)
            nc.vector.quantize_mx(
                out=codes[key][:, cols].bitcast(FP8X4),
                scales=scales[key][:, cols],
                in_=grouped[key][:, first_word * PACK : (first_word + words) * PACK],
            )

        for name in ("w_r0", "w_r1", "u_r", "w0", "w1", "u"):
            operand_tiles(name, name, D)
        for g in range(GROUPS):
            operand_tiles(("m", g), "m%d" % g, M_PASSES * GROUP_ROWS)
            operand_tiles(("h", g), "h%d" % g, GROUP_ROWS)
            operand_tiles(("rh", g), "rh%d" % g, GROUP_ROWS)

        def regroup_gate_weight(name):
            for half, copy in ((0, nc.vector.tensor_copy), (1, nc.scalar.copy)):
                cols = slice(half * HALF, (half + 1) * HALF)
                copy(
                    out=grouped[name][:, half * HALF * PACK : (half + 1) * HALF * PACK].rearrange(
                        "p (e q t) -> p q e t", e=2, t=PACK
                    ),
                    in_=raw[name][:, :, cols].rearrange("p t (q e) -> p q e t", e=2),
                )

        def regroup_candidate_weight(name, copy, first_col, cols):
            copy(
                out=grouped[name][:, first_col * PACK : (first_col + cols) * PACK].rearrange(
                    "p (c i t) -> p c t i", i=4, t=PACK
                ),
                in_=raw[name][:, :, first_col : first_col + cols].rearrange("p t (c i) -> p c t i", i=4),
            )

        def regroup_plainly(name, copy, first_col, cols):
            copy(
                out=grouped[name][:, first_col * PACK : (first_col + cols) * PACK].rearrange(
                    "p (c t) -> p c t", t=PACK
                ),
                in_=raw[name][:, :, first_col : first_col + cols].rearrange("p t c -> p c t"),
            )

        def flip(source, first_word, target_words):
            flipped = banks.tile([P, 2, GROUP_ROWS], F32, name="flipped", tag="bank")
            words = source[:].bitcast(F32)
            for j in range(GROUP_TILES):
                for half in range(2):
                    start = first_word + half * P
                    nc.tensor.transpose(
                        flipped[:, half, j * P : (j + 1) * P], words[:, j, start : start + P], ident[:]
                    )
            nc.scalar.copy(
                out=target_words.rearrange("p (r u) -> p r u", u=2),
                in_=flipped[:].rearrange("p u r -> p r u"),
            )

        def flip_message(g):
            words = grouped["m", g][:].bitcast(F32)
            for c in range(M_PASSES):
                flip(raw["m", g], c * HALF, words[:, c * 2 * GROUP_ROWS : (c + 1) * 2 * GROUP_ROWS])

        def flip_state(g):
            flip(raw["h", g], 0, grouped["h", g][:].bitcast(F32))

        def quantise_inputs(g):
            quantise(("m", g), 0, M_PASSES * GROUP_ROWS)
            quantise(("h", g), 0, GROUP_ROWS)

        gate = {}
        gate_acc = {}
        issued = set()

        def mx_pass(acc, stationary, s_cols, moving, m_cols, start, stop):
            nc.tensor.matmul_mx(
                out=acc,
                lhsT=codes[stationary][:, s_cols].bitcast(FP8X4),
                lhsT_scale=scales[stationary][:, s_cols],
                rhs=codes[moving][:, m_cols].bitcast(FP8X4),
                rhs_scale=scales[moving][:, m_cols],
                start=start,
                stop=stop,
            )

        def gate_pass(g, half, e, c):
            if (g, half) not in gate_acc:
                gate_acc[g, half] = banks.tile([P, 2, GROUP_ROWS], F32, name="gate_acc", tag="bank")
            feats = slice((2 * half + e) * P, (2 * half + e + 1) * P)
            acc = gate_acc[g, half][:, e, :]
            if c < M_PASSES:
                rows = slice(c * GROUP_ROWS, (c + 1) * GROUP_ROWS)
                mx_pass(acc, "w_r%d" % c, feats, ("m", g), rows, c == 0, False)
            else:
                mx_pass(acc, "u_r", feats, ("h", g), slice(0, GROUP_ROWS), False, True)
            issued.add((g, half, e, c))

        def finish_gate(g, half):
            if g not in gate:
                gate[g] = keep.tile([P, 2, GROUP_ROWS, 2], F32, name="gate%d" % g, align_bytes=512)
            for e in range(2):
                for c in range(M_PASSES + 1):
                    if (g, half, e, c) not in issued:
                        gate_pass(g, half, e, c)
            nc.scalar.activation(
                out=gate[g][:, half, :, :],
                in_=gate_acc[g, half][:].rearrange("p e r -> p r e"),
                func=SIGMOID,
            )

        def multiply(g, first_row, rows):
            cols = slice(first_row * PACK, (first_row + rows) * PACK)
            nc.vector.tensor_tensor(
                out=grouped["rh", g][:, cols].rearrange("p (r u e) -> p r u e", u=2, e=2),
                in0=gate[g][:, :, first_row : first_row + rows, :].rearrange("p u r e -> p r u e"),
                in1=grouped["h", g][:, cols].rearrange("p (r u e) -> p r u e", u=2, e=2),
                op=MULT,
            )

        def gated_state(g):
            for j in range(GROUP_TILES):
                multiply(g, j * P, P)
            for j in range(GROUP_TILES):
                quantise(("rh", g), j * P, P)

        cand_acc = {}

        def open_candidate(n):
            g, j = divmod(n, GROUP_TILES)
            cand_acc[n] = banks.tile([P, D], F32, name="cand_acc", tag="bank")
            for c in range(M_PASSES):
                rows = slice(c * GROUP_ROWS + j * P, c * GROUP_ROWS + (j + 1) * P)
                mx_pass(cand_acc[n][:], ("m", g), rows, "w%d" % c, slice(0, D), c == 0, False)

        def close_candidate(n):
            g, j = divmod(n, GROUP_TILES)
            rows = slice(j * P, (j + 1) * P)
            mx_pass(cand_acc[n][:], ("rh", g), rows, "u", slice(0, D), False, True)
            result = keep.tile([P, D], F32, name="result%d" % n)
            nc.scalar.activation(out=result[:], in_=cand_acc[n][:], func=TANH)
            nc.sync.dma_start(out=out_rows[:, g, j, :], in_=result[:])

        def last_candidate(n):
            g, j = divmod(n, GROUP_TILES)
            for half in range(2):
                cols = slice(half * HALF, (half + 1) * HALF)
                acc = banks.tile([P, HALF], F32, name="half_acc", tag="bank")
                for c in range(M_PASSES):
                    rows = slice(c * GROUP_ROWS + j * P, c * GROUP_ROWS + (j + 1) * P)
                    mx_pass(acc[:], ("m", g), rows, "w%d" % c, cols, c == 0, False)
                mx_pass(acc[:], ("rh", g), slice(j * P, (j + 1) * P), "u", cols, False, True)
                result = keep.tile([P, HALF], F32, name="result%d_%d" % (n, half))
                nc.scalar.activation(out=result[:], in_=acc[:], func=TANH)
                nc.sync.dma_start(out=out_rows[:, g, j, cols], in_=result[:])

        warm_up_tensor_engine(EARLY_WARM_UP_MATMULS)
        regroup_gate_weight("w_r0")
        flip_message(0)
        quantise("w_r0", 0, HALF)
        quantise("w_r0", HALF, HALF)
        regroup_gate_weight("w_r1")
        warm_up_tensor_engine(WARM_UP_MATMULS)
        flip_state(0)
        warm_up_tensor_engine(WARM_UP_MATMULS)
        quantise(("m", 0), 0, M_PASSES * GROUP_ROWS)
        gate_pass(0, 0, 0, 0)
        gate_pass(0, 1, 0, 0)
        quantise("w_r1", 0, HALF)
        gate_pass(0, 0, 0, 1)
        regroup_gate_weight("u_r")
        quantise("w_r1", HALF, HALF)
        quantise(("h", 0), 0, GROUP_ROWS)
        quantise("u_r", 0, HALF)
        warm_up_tensor_engine(WARM_UP_MATMULS + 1)
        flip_message(1)
        flip_state(1)
        quantise("u_r", HALF, HALF)

        for i in range(GROUPS - 1):
            finish_gate(i, 0)
            finish_gate(i, 1)
            if i + 2 < GROUPS:
                flip_message(i + 2)
                flip_state(i + 2)
                regroup_candidate_weight("w%d" % i, nc.vector.tensor_copy, 0, D)
                quantise_inputs(i + 1)
                quantise("w%d" % i, 0, D)
            if i == 1:
                multiply(0, 0, GROUP_ROWS)
                regroup_plainly("u", nc.scalar.copy, HALF, HALF)
        quantise_inputs(GROUPS - 1)
        open_candidate(0)
        open_candidate(1)
        regroup_candidate_weight("u", nc.vector.tensor_copy, 0, HALF)
        quantise(("rh", 0), 0, GROUP_ROWS)
        quantise("u", 0, D)
        finish_gate(GROUPS - 1, 0)
        finish_gate(GROUPS - 1, 1)
        for g in range(1, GROUPS):
            gated_state(g)

        last = ROW_TILES - 1
        for n in range(last):
            close_candidate(n)
            if n + 2 < last:
                open_candidate(n + 2)
        last_candidate(last)
